import numpy as np
import ml_dtypes


def mxq(x, axis, fmt="e4m3"):
    dtype, down = {"e4m3": (ml_dtypes.float8_e4m3fn, 7), "e5m2": (ml_dtypes.float8_e5m2, 14)}[fmt]
    v = np.moveaxis(np.asarray(x, np.float32).astype(ml_dtypes.bfloat16).astype(np.float64), axis, -1)
    blocks = v.reshape(v.shape[:-1] + (-1, 32))
    amax = np.abs(blocks).max(-1, keepdims=True)
    byte = np.maximum(np.where(amax > 0, np.frexp(amax)[1] - 1 + 127, 0) - down, 1)
    scale = np.exp2(byte - 127.0)
    codes = (blocks / scale).astype(np.float32).astype(dtype).astype(np.float64)
    return np.moveaxis((codes * scale).reshape(v.shape), -1, axis)


WIDE = False


def mx_kscale(k):
    if not WIDE:
        return np.ones(k)
    levels = np.array([10, -10, 5, -5, 0])
    a = np.random.permutation(np.resize(levels, k // 512 * 4)).reshape(k // 512, 4)
    idx = np.arange(k)
    return np.exp2(a[idx // 512, idx % 128 // 32])


BF16 = ml_dtypes.bfloat16


def bf(x):
    return np.asarray(x, np.float32).astype(BF16)


def f64(x):
    return np.asarray(x).astype(np.float64)


NS, GH, GW, DI, DO, NO = 8, 32, 32, 512, 1024, 128
HW = GH * GW
NIN = NS * HW
EPS = 1e-8


def squash(s):
    n2 = np.sum(s * s, axis=-1, keepdims=True)
    return (n2 / (1.0 + n2)) * s / np.sqrt(n2 + EPS)


def softmax(z):
    e = np.exp(z - z.max(axis=-1, keepdims=True))
    return e / e.sum(axis=-1, keepdims=True)


def setup_inputs():
    k = mx_kscale(DI)
    a = NO * np.sqrt(3.0 / (np.e * DO * NIN))
    u = np.random.standard_normal((NS, HW, DI)) * k
    return {"x": bf(u.reshape(1, NS * DI, GH, GW)),
            "W": bf(np.random.standard_normal((NS, DO, DI)) * a / np.sqrt(DI) / k),
            "b": bf(np.random.standard_normal((NIN, NO)))}


def reference(x, W, b):
    u = f64(x).reshape(NS, HW, DI)
    pred = mxq(u, 2, "e4m3") @ mxq(f64(W), 2, "e4m3").transpose(0, 2, 1)
    pred = pred.reshape(NIN, DO)
    c = softmax(f64(b))
    s = mxq(c, 0, "e4m3").T @ mxq(pred, 0, "e4m3")
    return squash(s)

@@ -1,0 +1,327 @@
+from contextlib import ExitStack
+
+import concourse.mybir as mybir
+from concourse.masks import make_identity
+
+F32 = mybir.dt.float32
+BF16 = mybir.dt.bfloat16
+U32 = mybir.dt.uint32
+U8 = mybir.dt.uint8
+FP8X4 = mybir.dt.float8_e4m3fn_x4
+ACTF = mybir.ActivationFunctionType
+ALU = mybir.AluOpType
+AX = mybir.AxisListType
+
+P = 128
+NS, HW, DI, DO, NO = 8, 1024, 512, 1024, 128
+NIN = NS * HW
+EPS = 1e-8
+FLOPS = 2 * NS * HW * DO * DI + 2 * NIN * NO * DO
+
+MANUAL = True
+NB = 16
+NPREP = 32
+NSLOT = 32
+NUNIT = 16
+HEAD_UNITS = 8
+M2LAG = 3
+EXP_T0 = 2
+EXP_NUM = 13
+TAIL_T = 29
+
+
+def tile_routing_t_kernel(tc, x, W, b, out):
+    nc = tc.nc
+    xv = x.rearrange("o c h w -> (o c h w)").rearrange("(g A p r) -> g A p r", g=NS, A=2, p=P)
+    wv = W.rearrange("g (A p a) f -> g A p (a f)", A=2, p=P)
+    bv = b.rearrange("(q G p j) o -> q p G (j o)", q=4, G=4, p=P)
+
+    with ExitStack() as ctx:
+        const = ctx.enter_context(tc.tile_pool(name="const", bufs=1))
+        inpool = ctx.enter_context(tc.tile_pool(name="inpool", bufs=NB))
+        bpool = ctx.enter_context(tc.tile_pool(name="bpool", bufs=4))
+        epool = ctx.enter_context(tc.tile_pool(name="epool", bufs=8))
+        small = ctx.enter_context(tc.tile_pool(name="small", bufs=8))
+        mpool = ctx.enter_context(tc.tile_pool(name="mpool", bufs=1))
+        cgpool = ctx.enter_context(tc.tile_pool(name="cgpool", bufs=8))
+        grpool = ctx.enter_context(tc.tile_pool(name="grpool", bufs=3))
+        copool = ctx.enter_context(tc.tile_pool(name="copool", bufs=8))
+        pgpool = ctx.enter_context(tc.tile_pool(name="pgpool", bufs=3))
+        pcpool = ctx.enter_context(tc.tile_pool(name="pcpool", bufs=5))
+        psacc = ctx.enter_context(tc.psum_pool(name="psacc", bufs=1))
+        psb = ctx.enter_context(tc.psum_pool(name="psb", bufs=6))
+        if MANUAL:
+            ctx.enter_context(tc.manual_schedule())
+
+        ident = const.tile([P, P], F32, name="ident")
+        ccodes = const.tile([P, NUNIT * P], U32, name="ccodes", align_bytes=64)
+        cplane = const.tile([P, NUNIT * P], U8, name="cplane", align_bytes=64)
+        out_sb = const.tile([P, DO], F32, name="out_sb")
+        junk = const.tile([P, 512], F32, name="junk")
+        dum = const.tile([P, 1], F32, name="dum")
+        dum2 = const.tile([P, 1], F32, name="dum2")
+        s_acc = [psacc.tile([P, 512], F32, name="s_acc%d" % a) for a in range(2)]
+
+        xin = {}
+        bsb = {}
+        grp = {}
+        cod = {}
+        pln = {}
+        pgt = {}
+        pcd = {}
+        ppl = {}
+        nmx = {}
+        sums = {}
+        etl = {}
+        cgt = {}
+
+        def prep_src(p):
+            g, r = divmod(p, 4)
+            return (xv[g, 0], wv[g, 0], wv[g, 1], xv[g, 1])[r]
+
+        def load(p):
+            t = inpool.tile([P, 2048], BF16, name="xin%d" % p, tag="xin")
+            nc.sync.dma_start(out=t[:], in_=prep_src(p))
+            xin[p] = t
+
+        def load_b(q, cuts):
+            t = bpool.tile([P, 2048], BF16, name="bsb%d" % q, tag="bsb")
+            tv = t[:].rearrange("p (G r) -> p G r", G=4)
+            for lo, hi in cuts:
+                nc.sync.dma_start(out=tv[:, lo:hi, :], in_=bv[q][:, lo:hi, :])
+            bsb[q] = t
+
+        def prep_t(p):
+            xf = xin[p][:].bitcast(F32)
+            gt = grpool.tile([P, 2048], BF16, name="grp%d" % p, tag="grp", align_bytes=64)
+            grp[p] = gt
+            gf = gt[:].bitcast(F32).rearrange("p (c u) -> p c u", u=2)
+            for bb in range(2):
+                xt = psb.tile([P, 512], F32, name="xt%d_%d" % (p, bb), tag="bank")
+                for aa in range(2):
+                    for u2 in range(2):
+                        a = 2 * bb + aa
+                        nc.tensor.transpose(
+                            xt[:, u2 * 256 + aa * P: u2 * 256 + aa * P + P],
+                            xf[:, a * 256 + u2 * P: a * 256 + u2 * P + P],
+                            ident[:],
+                        )
+                nc.vector.tensor_copy(
+                    out=gf[:, bb * 256:(bb + 1) * 256, :],
+                    in_=xt[:].rearrange("p (u c) -> p c u", u=2),
+                )
+
+        def q1(p):
+            ct = copool.tile([P, 512], U32, name="cod%d" % p, tag="cod", align_bytes=64)
+            pt = copool.tile([P, 512], U8, name="pln%d" % p, tag="pln", align_bytes=64)
+            nc.vector.quantize_mx(out=ct[:].bitcast(FP8X4), scales=pt[:], in_=grp[p][:])
+            cod[p] = ct
+            pln[p] = pt
+
+        def slot_ops(s):
+            g, r = divmod(s, 4)
+            au, aw = ((0, 0), (0, 1), (1, 1), (1, 0))[r]
+            pu = 4 * g + (0, 3)[au]
+            pw = 4 * g + (1, 2)[aw]
+            return g, au, aw, pu, pw
+
+        def mx1(s, evac):
+            g, au, aw, pu, pw = slot_ops(s)
+            pg = pgpool.tile([P, 2048], BF16, name="pg%d" % s, tag="pg", align_bytes=64)
+            pgt[s] = pg
+            for nq in range(4):
+                pp = psb.tile([P, 512], F32, name="pp%d_%d" % (s, nq), tag="bank")
+                for j in range(4):
+                    nc.tensor.matmul_mx(
+                        out=pp[:, j * P:(j + 1) * P],
+                        lhsT=cod[pu][:, j * P:(j + 1) * P].bitcast(FP8X4),
+                        lhsT_scale=pln[pu][:, j * P:(j + 1) * P],
+                        rhs=cod[pw][:, nq * P:(nq + 1) * P].bitcast(FP8X4),
+                        rhs_scale=pln[pw][:, nq * P:(nq + 1) * P],
+                        start=True,
+                        stop=True,
+                    )
+                dst = pg[:, nq * 512:(nq + 1) * 512].rearrange("p (n j) -> p n j", j=4)
+                src = pp[:].rearrange("p (j n) -> p n j", j=4)
+                if evac[nq] == "a":
+                    nc.scalar.copy(out=dst, in_=src)
+                else:
+                    nc.vector.tensor_copy(out=dst, in_=src)
+
+        def q2(s):
+            ct = pcpool.tile([P, 512], U32, name="pcd%d" % s, tag="pcd", align_bytes=64)
+            pt = pcpool.tile([P, 512], U8, name="ppl%d" % s, tag="ppl", align_bytes=64)
+            nc.vector.quantize_mx(out=ct[:].bitcast(FP8X4), scales=pt[:], in_=pgt[s][:])
+            pcd[s] = ct
+            ppl[s] = pt
+
+        def mx2(s):
+            g, au, aw, pu, pw = slot_ops(s)
+            un = 2 * g + au
+            nc.tensor.matmul_mx(
+                out=s_acc[aw][:],
+                lhsT=ccodes[:, un * P:(un + 1) * P].bitcast(FP8X4),
+                lhsT_scale=cplane[:, un * P:(un + 1) * P],
+                rhs=pcd[s][:].bitcast(FP8X4),
+                rhs_scale=ppl[s][:],
+                start=(un == 0),
+                stop=(un == NUNIT - 1),
+            )
+
+        def b_unit(un):
+            q, gl = divmod(un, 4)
+            return bsb[q][:, gl * 512:(gl + 1) * 512]
+
+        def sm_tiles(un):
+            sums[un] = small.tile([P, 4], F32, name="sums%d" % un, tag="sums")
+            etl[un] = epool.tile([P, 512], F32, name="etl%d" % un, tag="etl")
+
+        def sm_max(un):
+            nm = small.tile([P, 4], F32, name="nmx%d" % un, tag="nmx")
+            nc.vector.tensor_reduce(
+                out=nm[:], in_=b_unit(un).rearrange("p (r o) -> p r o", o=NO),
+                axis=AX.X, op=ALU.max, negate=True,
+            )
+            nmx[un] = nm[:]
+            sm_tiles(un)
+
+        def sm_max_chunk(q):
+            bs = bsb[q][:].rearrange("p (r o) -> p r o", o=NO)
+            m1 = mpool.tile([P, 16, 64], BF16, name="m1_%d" % q, tag="m1")
+            m2 = mpool.tile([P, 16, 32], BF16, name="m2_%d" % q, tag="m2")
+            m3 = mpool.tile([P, 16, 16], BF16, name="m3_%d" % q, tag="m3")
+            nm = small.tile([P, 16], F32, name="nmc%d" % q, tag="nmc", bufs=2)
+            nc.vector.tensor_tensor(out=m1[:], in0=bs[:, :, 0:64], in1=bs[:, :, 64:128], op=ALU.max)
+            nc.vector.tensor_tensor(out=m2[:], in0=m1[:, :, 0:32], in1=m1[:, :, 32:64], op=ALU.max)
+            nc.vector.tensor_tensor(out=m3[:], in0=m2[:, :, 0:16], in1=m2[:, :, 16:32], op=ALU.max)
+            nc.vector.tensor_reduce(out=nm[:], in_=m3[:], axis=AX.X, op=ALU.max, negate=True)
+            for gl in range(4):
+                nmx[4 * q + gl] = nm[:, 4 * gl:4 * gl + 4]
+
+        def sm_exp(un, j):
+            if un not in etl:
+                sm_tiles(un)
+            nc.scalar.activation(
+                out=etl[un][:, j * NO:(j + 1) * NO], in_=b_unit(un)[:, j * NO:(j + 1) * NO],
+                func=ACTF.Exp, bias=nmx[un][:, j:j + 1], scale=1.0,
+                accum_out=sums[un][:, j:j + 1],
+            )
+
+        def sm_norm(un):
+            rs = small.tile([P, 4], F32, name="rs%d" % un, tag="rs")
+            nc.vector.reciprocal(out=rs[:], in_=sums[un][:])
+            cg = cgpool.tile([P, 512], BF16, name="cg%d" % un, tag="cg", align_bytes=64)
+            nc.gpsimd.tensor_tensor(
+                out=cg[:].rearrange("p (o j) -> p o j", j=4),
+                in0=etl[un][:].rearrange("p (j o) -> p o j", j=4),
+                in1=rs[:].unsqueeze(1).to_broadcast([P, NO, 4]),
+                op=ALU.mult,
+            )
+            cgt[un] = cg
+
+        def sm_q(un):
+            nc.vector.quantize_mx(
+                out=ccodes[:, un * P:(un + 1) * P].bitcast(FP8X4),
+                scales=cplane[:, un * P:(un + 1) * P],
+                in_=cgt[un][:],
+            )
+
+        pre_fill = {}
+        dve_fill = {}
+        act_fill = {}
+
+        def add(d, t, item):
+            if t not in d:
+                d[t] = []
+            d[t].append(item)
+
+        for un in range(HEAD_UNITS):
+            add(pre_fill, (-3, -3, -2, -2, -1, 0, 1, 2)[un], un)
+            add(dve_fill, (0, 0, 1, 1, 2, 3, 4, 5)[un], ("q", un))
+        for un in range(HEAD_UNITS, NUNIT):
+            first = 4 * (un - HEAD_UNITS)
+            if un % 4 == 0:
+                add(dve_fill, EXP_T0 + (first * EXP_NUM) // 16 - 2, ("maxc", un // 4))
+            for j in range(4):
+                add(act_fill, EXP_T0 + ((first + j) * EXP_NUM) // 16, (un, j))
+            tl = EXP_T0 + ((first + 3) * EXP_NUM) // 16
+            add(pre_fill, tl + 3, un)
+            add(dve_fill, tl + 4, ("q", un))
+        last_exp_t = EXP_T0 + ((4 * (NUNIT - HEAD_UNITS) - 1) * EXP_NUM) // 16
+
+        nc.vector.memset(dum[:], 1.0)
+        nc.scalar.activation(out=dum2[:], in_=dum[:], func=ACTF.Exp)
+        make_identity(nc, ident[:])
+        load_b(0, ((0, 1), (1, 4)))
+        load_b(1, ((0, 4),))
+        for p in range(4):
+            load(p)
+        load_b(2, ((0, 4),))
+        for p in range(4, 8):
+            load(p)
+        load_b(3, ((0, 4),))
+        for p in range(8, NB):
+            load(p)
+        for un in range(4):
+            sm_max(un)
+            for j in range(4):
+                sm_exp(un, j)
+        sm_max_chunk(1)
+        for un in range(4, HEAD_UNITS):
+            for j in range(4):
+                sm_exp(un, j)
+
+        n2 = [const.tile([P, 1], F32, name="n2_%d" % a) for a in range(2)]
+
+        for t in range(-3, NSLOT + M2LAG):
+            for un in pre_fill.get(t, []):
+                sm_norm(un)
+            if t < 0 and 0 <= t + 2:
+                q1(t + 2)
+            if 0 <= t + 3 < NPREP:
+                prep_t(t + 3)
+                if t + 3 + NB < NPREP:
+                    load(t + 3 + NB)
+            if 0 <= t - M2LAG < NSLOT:
+                mx2(t - M2LAG)
+                if t - M2LAG == NSLOT - 2:
+                    nc.scalar.activation(out=junk[:], in_=s_acc[1][:], func=ACTF.Square, accum_out=n2[1][:])
+            for un, j in act_fill.get(t, []):
+                sm_exp(un, j)
+            if t == last_exp_t:
+                nc.scalar.activation(out=dum2[:], in_=dum[:], func=ACTF.Sqrt)
+            if t >= TAIL_T and 0 <= t - 1 < NSLOT:
+                q2(t - 1)
+            if 0 <= t < NSLOT:
+                mx1(t, "aaaa" if t < TAIL_T else "avav")
+            if t >= 0 and t + 2 < NPREP:
+                q1(t + 2)
+            for kind, un in dve_fill.get(t, []):
+                if kind == "maxc":
+                    sm_max_chunk(un)
+                else:
+                    sm_q(un)
+            if t < TAIL_T and 0 <= t - 1 < NSLOT:
+                q2(t - 1)
+
+        nc.scalar.activation(out=junk[:], in_=s_acc[0][:], func=ACTF.Square, accum_out=n2[0][:])
+        t1 = const.tile([P, 1], F32, name="t1")
+        n2s = const.tile([P, 1], F32, name="n2s")
+        rt = const.tile([P, 1], F32, name="rt")
+        den = const.tile([P, 1], F32, name="den")
+        rec = const.tile([P, 1], F32, name="rec")
+        fac = const.tile([P, 1], F32, name="fac")
+        nc.vector.scalar_tensor_tensor(out=t1[:], in0=n2[0][:], scalar=EPS, in1=n2[1][:], op0=ALU.add, op1=ALU.add)
+        nc.scalar.activation(out=rt[:], in_=t1[:], func=ACTF.Sqrt)
+        nc.vector.tensor_tensor(out=n2s[:], in0=n2[0][:], in1=n2[1][:], op=ALU.add)
+        nc.vector.scalar_tensor_tensor(out=den[:], in0=n2s[:], scalar=1.0, in1=rt[:], op0=ALU.add, op1=ALU.mult)
+        nc.vector.reciprocal(out=rec[:], in_=den[:])
+        nc.vector.tensor_tensor(out=fac[:], in0=n2s[:], in1=rec[:], op=ALU.mult)
+        for a in range(2):
+            dst = out_sb[:, a * 512:(a + 1) * 512].rearrange("p (c q) -> p c q", q=4)
+            src = s_acc[a][:].rearrange("p (q c) -> p c q", q=4)
+            if a == 0:
+                nc.scalar.activation(out=dst, in_=src, func=ACTF.Copy, scale=fac[:, 0:1])
+            else:
+                nc.vector.tensor_scalar(out=dst, in0=src, scalar1=fac[:, 0:1], scalar2=None, op0=ALU.mult)
+            nc.sync.dma_start(out=out[:, a * 512:(a + 1) * 512], in_=out_sb[:, a * 512:(a + 1) * 512])

@@ -18,7 +18,7 @@ NIN = NS * HW
 EPS = 1e-8
 FLOPS = 2 * NS * HW * DO * DI + 2 * NIN * NO * DO
 
-MANUAL = True
+MANUAL = False
 NB = 16
 NPREP = 32
 NSLOT = 32

@@ -18,7 +18,8 @@ NIN = NS * HW
 EPS = 1e-8
 FLOPS = 2 * NS * HW * DO * DI + 2 * NIN * NO * DO
 
-MANUAL = False
+MANUAL = True
+PE_ANY = False
 NB = 16
 NPREP = 32
 NSLOT = 32
@@ -26,8 +27,10 @@ NUNIT = 16
 HEAD_UNITS = 8
 M2LAG = 3
 EXP_T0 = 2
-EXP_NUM = 13
+EXP_NUM = 12
 TAIL_T = 29
+TE_ACT_EVERY = 1000
+STRIDED_OUT = False
 
 
 def tile_routing_t_kernel(tc, x, W, b, out):
@@ -106,10 +109,16 @@ def tile_routing_t_kernel(tc, x, W, b, out):
                             xf[:, a * 256 + u2 * P: a * 256 + u2 * P + P],
                             ident[:],
                         )
-                nc.vector.tensor_copy(
-                    out=gf[:, bb * 256:(bb + 1) * 256, :],
-                    in_=xt[:].rearrange("p (u c) -> p c u", u=2),
-                )
+                if bb == 1 and p % TE_ACT_EVERY == TE_ACT_EVERY - 1:
+                    nc.scalar.copy(
+                        out=gf[:, bb * 256:(bb + 1) * 256, :],
+                        in_=xt[:].rearrange("p (u c) -> p c u", u=2),
+                    )
+                else:
+                    nc.vector.tensor_copy(
+                        out=gf[:, bb * 256:(bb + 1) * 256, :],
+                        in_=xt[:].rearrange("p (u c) -> p c u", u=2),
+                    )
 
         def q1(p):
             ct = copool.tile([P, 512], U32, name="cod%d" % p, tag="cod", align_bytes=64)
@@ -133,7 +142,7 @@ def tile_routing_t_kernel(tc, x, W, b, out):
                 pp = psb.tile([P, 512], F32, name="pp%d_%d" % (s, nq), tag="bank")
                 for j in range(4):
                     nc.tensor.matmul_mx(
-                        out=pp[:, j * P:(j + 1) * P],
+                        out=(pp[:].rearrange("p (n j) -> p j n", j=4)[:, j, :] if STRIDED_OUT else pp[:, j * P:(j + 1) * P]),
                         lhsT=cod[pu][:, j * P:(j + 1) * P].bitcast(FP8X4),
                         lhsT_scale=pln[pu][:, j * P:(j + 1) * P],
                         rhs=cod[pw][:, nq * P:(nq + 1) * P].bitcast(FP8X4),
@@ -141,9 +150,15 @@ def tile_routing_t_kernel(tc, x, W, b, out):
                         start=True,
                         stop=True,
                     )
-                dst = pg[:, nq * 512:(nq + 1) * 512].rearrange("p (n j) -> p n j", j=4)
-                src = pp[:].rearrange("p (j n) -> p n j", j=4)
-                if evac[nq] == "a":
+                if STRIDED_OUT:
+                    dst = pg[:, nq * 512:(nq + 1) * 512]
+                    src = pp[:]
+                else:
+                    dst = pg[:, nq * 512:(nq + 1) * 512].rearrange("p (n j) -> p n j", j=4)
+                    src = pp[:].rearrange("p (j n) -> p n j", j=4)
+                if PE_ANY:
+                    nc.any.tensor_copy(out=dst, in_=src)
+                elif evac[nq] == "a":
                     nc.scalar.copy(out=dst, in_=src)
                 else:
                     nc.vector.tensor_copy(out=dst, in_=src)
@@ -185,18 +200,19 @@ def tile_routing_t_kernel(tc, x, W, b, out):
             nmx[un] = nm[:]
             sm_tiles(un)
 
-        def sm_max_chunk(q):
-            bs = bsb[q][:].rearrange("p (r o) -> p r o", o=NO)
+        def sm_max_chunk(q, lo=0):
+            nr = 4 * (4 - lo)
+            bs = bsb[q][:, lo * 512:2048].rearrange("p (r o) -> p r o", o=NO)
             m1 = mpool.tile([P, 16, 64], BF16, name="m1_%d" % q, tag="m1")
             m2 = mpool.tile([P, 16, 32], BF16, name="m2_%d" % q, tag="m2")
             m3 = mpool.tile([P, 16, 16], BF16, name="m3_%d" % q, tag="m3")
-            nm = small.tile([P, 16], F32, name="nmc%d" % q, tag="nmc", bufs=2)
-            nc.vector.tensor_tensor(out=m1[:], in0=bs[:, :, 0:64], in1=bs[:, :, 64:128], op=ALU.max)
-            nc.vector.tensor_tensor(out=m2[:], in0=m1[:, :, 0:32], in1=m1[:, :, 32:64], op=ALU.max)
-            nc.vector.tensor_tensor(out=m3[:], in0=m2[:, :, 0:16], in1=m2[:, :, 16:32], op=ALU.max)
-            nc.vector.tensor_reduce(out=nm[:], in_=m3[:], axis=AX.X, op=ALU.max, negate=True)
-            for gl in range(4):
-                nmx[4 * q + gl] = nm[:, 4 * gl:4 * gl + 4]
+            nm = small.tile([P, 16], F32, name="nmc%d" % q, tag="nmc", bufs=3)
+            nc.vector.tensor_tensor(out=m1[:, 0:nr, :], in0=bs[:, :, 0:64], in1=bs[:, :, 64:128], op=ALU.max)
+            nc.vector.tensor_tensor(out=m2[:, 0:nr, :], in0=m1[:, 0:nr, 0:32], in1=m1[:, 0:nr, 32:64], op=ALU.max)
+            nc.vector.tensor_tensor(out=m3[:, 0:nr, :], in0=m2[:, 0:nr, 0:16], in1=m2[:, 0:nr, 16:32], op=ALU.max)
+            nc.vector.tensor_reduce(out=nm[:, 0:nr], in_=m3[:, 0:nr, :], axis=AX.X, op=ALU.max, negate=True)
+            for gl in range(lo, 4):
+                nmx[4 * q + gl] = nm[:, 4 * (gl - lo):4 * (gl - lo) + 4]
 
         def sm_exp(un, j):
             if un not in etl:
@@ -236,8 +252,8 @@ def tile_routing_t_kernel(tc, x, W, b, out):
             d[t].append(item)
 
         for un in range(HEAD_UNITS):
-            add(pre_fill, (-3, -3, -2, -2, -1, 0, 1, 2)[un], un)
-            add(dve_fill, (0, 0, 1, 1, 2, 3, 4, 5)[un], ("q", un))
+            add(pre_fill, un - 3, un)
+            add(dve_fill, max(un - 2, 0), ("q", un))
         for un in range(HEAD_UNITS, NUNIT):
             first = 4 * (un - HEAD_UNITS)
             if un % 4 == 0:
@@ -262,8 +278,11 @@ def tile_routing_t_kernel(tc, x, W, b, out):
         load_b(3, ((0, 4),))
         for p in range(8, NB):
             load(p)
-        for un in range(4):
-            sm_max(un)
+        sm_max(0)
+        for j in range(4):
+            sm_exp(0, j)
+        sm_max_chunk(0, 1)
+        for un in range(1, 4):
             for j in range(4):
                 sm_exp(un, j)
         sm_max_chunk(1)
@@ -272,10 +291,12 @@ def tile_routing_t_kernel(tc, x, W, b, out):
                 sm_exp(un, j)
 
         n2 = [const.tile([P, 1], F32, name="n2_%d" % a) for a in range(2)]
+        n1e = const.tile([P, 1], F32, name="n1e")
 
         for t in range(-3, NSLOT + M2LAG):
-            for un in pre_fill.get(t, []):
-                sm_norm(un)
+            if t <= 0:
+                for un in pre_fill.get(t, []):
+                    sm_norm(un)
             if t < 0 and 0 <= t + 2:
                 q1(t + 2)
             if 0 <= t + 3 < NPREP:
@@ -286,38 +307,45 @@ def tile_routing_t_kernel(tc, x, W, b, out):
                 mx2(t - M2LAG)
                 if t - M2LAG == NSLOT - 2:
                     nc.scalar.activation(out=junk[:], in_=s_acc[1][:], func=ACTF.Square, accum_out=n2[1][:])
+                    nc.vector.tensor_scalar(out=n1e[:], in0=n2[1][:], scalar1=EPS, scalar2=None, op0=ALU.add)
             for un, j in act_fill.get(t, []):
                 sm_exp(un, j)
             if t == last_exp_t:
-                nc.scalar.activation(out=dum2[:], in_=dum[:], func=ACTF.Sqrt)
-            if t >= TAIL_T and 0 <= t - 1 < NSLOT:
-                q2(t - 1)
-            if 0 <= t < NSLOT:
-                mx1(t, "aaaa" if t < TAIL_T else "avav")
-            if t >= 0 and t + 2 < NPREP:
-                q1(t + 2)
-            for kind, un in dve_fill.get(t, []):
-                if kind == "maxc":
-                    sm_max_chunk(un)
-                else:
-                    sm_q(un)
-            if t < TAIL_T and 0 <= t - 1 < NSLOT:
-                q2(t - 1)
+                nc.scalar.activation(out=dum2[:], in_=sums[NUNIT - 1][:, 3:4], func=ACTF.Sqrt)
+            late = t >= TAIL_T
+            for when in (True, False):
+                if late == when:
+                    if t >= 0 and t + 2 < NPREP:
+                        q1(t + 2)
+                    for kind, un in dve_fill.get(t, []):
+                        if kind == "maxc":
+                            sm_max_chunk(un)
+                        else:
+                            sm_q(un)
+                    if t >= 0:
+                        for un in pre_fill.get(t + 1, []):
+                            sm_norm(un)
+                    if 0 <= t - 1 < NSLOT:
+                        q2(t - 1)
+                if when and 0 <= t < NSLOT:
+                    mx1(t, "avav" if late else "aaaa")
 
         nc.scalar.activation(out=junk[:], in_=s_acc[0][:], func=ACTF.Square, accum_out=n2[0][:])
-        t1 = const.tile([P, 1], F32, name="t1")
-        n2s = const.tile([P, 1], F32, name="n2s")
         rt = const.tile([P, 1], F32, name="rt")
+        n2s = const.tile([P, 1], F32, name="n2s")
         den = const.tile([P, 1], F32, name="den")
-        rec = const.tile([P, 1], F32, name="rec")
+        rden = const.tile([P, 1], F32, name="rden")
+        mfac = const.tile([P, 1], F32, name="mfac")
+        rrt = const.tile([P, 1], F32, name="rrt")
         fac = const.tile([P, 1], F32, name="fac")
-        nc.vector.scalar_tensor_tensor(out=t1[:], in0=n2[0][:], scalar=EPS, in1=n2[1][:], op0=ALU.add, op1=ALU.add)
-        nc.scalar.activation(out=rt[:], in_=t1[:], func=ACTF.Sqrt)
+        nc.scalar.activation(out=rt[:], in_=n2[0][:], func=ACTF.Sqrt, bias=n1e[:, 0:1], scale=1.0)
         nc.vector.tensor_tensor(out=n2s[:], in0=n2[0][:], in1=n2[1][:], op=ALU.add)
-        nc.vector.scalar_tensor_tensor(out=den[:], in0=n2s[:], scalar=1.0, in1=rt[:], op0=ALU.add, op1=ALU.mult)
-        nc.vector.reciprocal(out=rec[:], in_=den[:])
-        nc.vector.tensor_tensor(out=fac[:], in0=n2s[:], in1=rec[:], op=ALU.mult)
-        for a in range(2):
+        nc.vector.tensor_scalar(out=den[:], in0=n2s[:], scalar1=1.0, scalar2=None, op0=ALU.add)
+        nc.vector.reciprocal(out=rden[:], in_=den[:])
+        nc.vector.tensor_tensor(out=mfac[:], in0=n2s[:], in1=rden[:], op=ALU.mult)
+        nc.vector.reciprocal(out=rrt[:], in_=rt[:])
+        nc.vector.tensor_tensor(out=fac[:], in0=mfac[:], in1=rrt[:], op=ALU.mult)
+        for a in (1, 0):
             dst = out_sb[:, a * 512:(a + 1) * 512].rearrange("p (c q) -> p c q", q=4)
             src = s_acc[a][:].rearrange("p (q c) -> p c q", q=4)
             if a == 0:

@@ -46,7 +46,7 @@ def tile_routing_t_kernel(tc, x, W, b, out):
         epool = ctx.enter_context(tc.tile_pool(name="epool", bufs=8))
         small = ctx.enter_context(tc.tile_pool(name="small", bufs=8))
         mpool = ctx.enter_context(tc.tile_pool(name="mpool", bufs=1))
-        cgpool = ctx.enter_context(tc.tile_pool(name="cgpool", bufs=8))
+        cgpool = ctx.enter_context(tc.tile_pool(name="cgpool", bufs=1))
         grpool = ctx.enter_context(tc.tile_pool(name="grpool", bufs=3))
         copool = ctx.enter_context(tc.tile_pool(name="copool", bufs=8))
         pgpool = ctx.enter_context(tc.tile_pool(name="pgpool", bufs=3))
@@ -77,6 +77,7 @@ def tile_routing_t_kernel(tc, x, W, b, out):
         sums = {}
         etl = {}
         cgt = {}
+        rcp = {}
 
         def prep_src(p):
             g, r = divmod(p, 4)
@@ -223,26 +224,29 @@ def tile_routing_t_kernel(tc, x, W, b, out):
                 accum_out=sums[un][:, j:j + 1],
             )
 
-        def sm_norm(un):
+        def sm_rec(un):
             rs = small.tile([P, 4], F32, name="rs%d" % un, tag="rs")
             nc.vector.reciprocal(out=rs[:], in_=sums[un][:])
-            cg = cgpool.tile([P, 512], BF16, name="cg%d" % un, tag="cg", align_bytes=64)
+            rcp[un] = rs
+
+        def sm_half(k):
+            un, h = divmod(k, 2)
+            cg = cgpool.tile([P, 256], BF16, name="cg%d" % k, tag="cg", align_bytes=64)
             nc.gpsimd.tensor_tensor(
                 out=cg[:].rearrange("p (o j) -> p o j", j=4),
-                in0=etl[un][:].rearrange("p (j o) -> p o j", j=4),
-                in1=rs[:].unsqueeze(1).to_broadcast([P, NO, 4]),
+                in0=etl[un][:].rearrange("p (j o) -> p o j", j=4)[:, h * 64:(h + 1) * 64, :],
+                in1=rcp[un][:].unsqueeze(1).to_broadcast([P, 64, 4]),
                 op=ALU.mult,
             )
-            cgt[un] = cg
+            cgt[k] = cg
 
-        def sm_q(un):
+        def sm_qh(k):
             nc.vector.quantize_mx(
-                out=ccodes[:, un * P:(un + 1) * P].bitcast(FP8X4),
-                scales=cplane[:, un * P:(un + 1) * P],
-                in_=cgt[un][:],
+                out=ccodes[:, k * 64:(k + 1) * 64].bitcast(FP8X4),
+                scales=cplane[:, k * 64:(k + 1) * 64],
+                in_=cgt[k][:],
             )
 
-        pre_fill = {}
         dve_fill = {}
         act_fill = {}
 
@@ -251,18 +255,12 @@ def tile_routing_t_kernel(tc, x, W, b, out):
                 d[t] = []
             d[t].append(item)
 
-        for un in range(HEAD_UNITS):
-            add(pre_fill, un - 3, un)
-            add(dve_fill, max(un - 2, 0), ("q", un))
         for un in range(HEAD_UNITS, NUNIT):
             first = 4 * (un - HEAD_UNITS)
             if un % 4 == 0:
                 add(dve_fill, EXP_T0 + (first * EXP_NUM) // 16 - 2, ("maxc", un // 4))
             for j in range(4):
                 add(act_fill, EXP_T0 + ((first + j) * EXP_NUM) // 16, (un, j))
-            tl = EXP_T0 + ((first + 3) * EXP_NUM) // 16
-            add(pre_fill, tl + 3, un)
-            add(dve_fill, tl + 4, ("q", un))
         last_exp_t = EXP_T0 + ((4 * (NUNIT - HEAD_UNITS) - 1) * EXP_NUM) // 16
 
         nc.vector.memset(dum[:], 1.0)
@@ -294,9 +292,8 @@ def tile_routing_t_kernel(tc, x, W, b, out):
         n1e = const.tile([P, 1], F32, name="n1e")
 
         for t in range(-3, NSLOT + M2LAG):
-            if t <= 0:
-                for un in pre_fill.get(t, []):
-                    sm_norm(un)
+            if t == -3:
+                sm_rec(0)
             if t < 0 and 0 <= t + 2:
                 q1(t + 2)
             if 0 <= t + 3 < NPREP:
@@ -318,13 +315,14 @@ def tile_routing_t_kernel(tc, x, W, b, out):
                     if t >= 0 and t + 2 < NPREP:
                         q1(t + 2)
                     for kind, un in dve_fill.get(t, []):
-                        if kind == "maxc":
-                            sm_max_chunk(un)
-                        else:
-                            sm_q(un)
-                    if t >= 0:
-                        for un in pre_fill.get(t + 1, []):
-                            sm_norm(un)
+                        sm_max_chunk(un)
+                    k = t + 3
+                    if 0 <= k - 1 < 2 * NUNIT:
+                        sm_qh(k - 1)
+                    if k % 2 == 1 and (k + 1) // 2 < NUNIT:
+                        sm_rec((k + 1) // 2)
+                    if k < 2 * NUNIT:
+                        sm_half(k)
                     if 0 <= t - 1 < NSLOT:
                         q2(t - 1)
                 if when and 0 <= t < NSLOT:

@@ -261,7 +261,6 @@ def tile_routing_t_kernel(tc, x, W, b, out):
                 add(dve_fill, EXP_T0 + (first * EXP_NUM) // 16 - 2, ("maxc", un // 4))
             for j in range(4):
                 add(act_fill, EXP_T0 + ((first + j) * EXP_NUM) // 16, (un, j))
-        last_exp_t = EXP_T0 + ((4 * (NUNIT - HEAD_UNITS) - 1) * EXP_NUM) // 16
 
         nc.vector.memset(dum[:], 1.0)
         nc.scalar.activation(out=dum2[:], in_=dum[:], func=ACTF.Exp)
@@ -307,8 +306,6 @@ def tile_routing_t_kernel(tc, x, W, b, out):
                     nc.vector.tensor_scalar(out=n1e[:], in0=n2[1][:], scalar1=EPS, scalar2=None, op0=ALU.add)
             for un, j in act_fill.get(t, []):
                 sm_exp(un, j)
-            if t == last_exp_t:
-                nc.scalar.activation(out=dum2[:], in_=sums[NUNIT - 1][:, 3:4], func=ACTF.Sqrt)
             late = t >= TAIL_T
             for when in (True, False):
                 if late == when:
@@ -327,6 +324,8 @@ def tile_routing_t_kernel(tc, x, W, b, out):
                         q2(t - 1)
                 if when and 0 <= t < NSLOT:
                     mx1(t, "avav" if late else "aaaa")
+                    if t == NSLOT - 1:
+                        nc.scalar.activation(out=dum2[:], in_=dum[:], func=ACTF.Sqrt)
 
         nc.scalar.activation(out=junk[:], in_=s_acc[0][:], func=ACTF.Square, accum_out=n2[0][:])
         rt = const.tile([P, 1], F32, name="rt")
@@ -343,11 +342,13 @@ def tile_routing_t_kernel(tc, x, W, b, out):
         nc.vector.tensor_tensor(out=mfac[:], in0=n2s[:], in1=rden[:], op=ALU.mult)
         nc.vector.reciprocal(out=rrt[:], in_=rt[:])
         nc.vector.tensor_tensor(out=fac[:], in0=mfac[:], in1=rrt[:], op=ALU.mult)
-        for a in (1, 0):
-            dst = out_sb[:, a * 512:(a + 1) * 512].rearrange("p (c q) -> p c q", q=4)
-            src = s_acc[a][:].rearrange("p (q c) -> p c q", q=4)
-            if a == 0:
-                nc.scalar.activation(out=dst, in_=src, func=ACTF.Copy, scale=fac[:, 0:1])
-            else:
-                nc.vector.tensor_scalar(out=dst, in0=src, scalar1=fac[:, 0:1], scalar2=None, op0=ALU.mult)
-            nc.sync.dma_start(out=out[:, a * 512:(a + 1) * 512], in_=out_sb[:, a * 512:(a + 1) * 512])
+        for h in range(2):
+            for a in (1, 0):
+                lo = a * 512 + h * 256
+                dst = out_sb[:, lo:lo + 256].rearrange("p (c q) -> p c q", q=4)
+                src = s_acc[a][:].rearrange("p (q c) -> p c q", q=4)[:, h * 64:(h + 1) * 64, :]
+                if a == 0:
+                    nc.scalar.activation(out=dst, in_=src, func=ACTF.Copy, scale=fac[:, 0:1])
+                else:
+                    nc.vector.tensor_scalar(out=dst, in0=src, scalar1=fac[:, 0:1], scalar2=None, op0=ALU.mult)
+                nc.sync.dma_start(out=out[:, lo:lo + 256], in_=out_sb[:, lo:lo + 256])

@@ -18,19 +18,11 @@ NIN = NS * HW
 EPS = 1e-8
 FLOPS = 2 * NS * HW * DO * DI + 2 * NIN * NO * DO
 
-MANUAL = True
-PE_ANY = False
 NB = 16
 NPREP = 32
 NSLOT = 32
 NUNIT = 16
-HEAD_UNITS = 8
 M2LAG = 3
-EXP_T0 = 2
-EXP_NUM = 12
-TAIL_T = 29
-TE_ACT_EVERY = 1000
-STRIDED_OUT = False
 
 
 def tile_routing_t_kernel(tc, x, W, b, out):
@@ -44,7 +36,7 @@ def tile_routing_t_kernel(tc, x, W, b, out):
         inpool = ctx.enter_context(tc.tile_pool(name="inpool", bufs=NB))
         bpool = ctx.enter_context(tc.tile_pool(name="bpool", bufs=4))
         epool = ctx.enter_context(tc.tile_pool(name="epool", bufs=8))
-        small = ctx.enter_context(tc.tile_pool(name="small", bufs=8))
+        small = ctx.enter_context(tc.tile_pool(name="small", bufs=4))
         mpool = ctx.enter_context(tc.tile_pool(name="mpool", bufs=1))
         cgpool = ctx.enter_context(tc.tile_pool(name="cgpool", bufs=1))
         grpool = ctx.enter_context(tc.tile_pool(name="grpool", bufs=3))
@@ -53,8 +45,7 @@ def tile_routing_t_kernel(tc, x, W, b, out):
         pcpool = ctx.enter_context(tc.tile_pool(name="pcpool", bufs=5))
         psacc = ctx.enter_context(tc.psum_pool(name="psacc", bufs=1))
         psb = ctx.enter_context(tc.psum_pool(name="psb", bufs=6))
-        if MANUAL:
-            ctx.enter_context(tc.manual_schedule())
+        ctx.enter_context(tc.manual_schedule())
 
         ident = const.tile([P, P], F32, name="ident")
         ccodes = const.tile([P, NUNIT * P], U32, name="ccodes", align_bytes=64)
@@ -63,45 +54,35 @@ def tile_routing_t_kernel(tc, x, W, b, out):
         junk = const.tile([P, 512], F32, name="junk")
         dum = const.tile([P, 1], F32, name="dum")
         dum2 = const.tile([P, 1], F32, name="dum2")
+        nmx = const.tile([P, 4 * NUNIT], F32, name="nmx")
         s_acc = [psacc.tile([P, 512], F32, name="s_acc%d" % a) for a in range(2)]
 
-        xin = {}
-        bsb = {}
-        grp = {}
-        cod = {}
-        pln = {}
-        pgt = {}
-        pcd = {}
-        ppl = {}
-        nmx = {}
-        sums = {}
-        etl = {}
-        cgt = {}
-        rcp = {}
+        xin, grp, cod, pln, pgt, pcd, ppl, bsb = {}, {}, {}, {}, {}, {}, {}, {}
+        sums, etl, cgt, rcp, tree, xts = {}, {}, {}, {}, {}, {}
 
         def prep_src(p):
             g, r = divmod(p, 4)
             return (xv[g, 0], wv[g, 0], wv[g, 1], xv[g, 1])[r]
 
-        def load(p):
+        def load(p, parts=1):
             t = inpool.tile([P, 2048], BF16, name="xin%d" % p, tag="xin")
-            nc.sync.dma_start(out=t[:], in_=prep_src(p))
+            w = 2048 // parts
+            for i in range(parts):
+                nc.sync.dma_start(out=t[:, i * w:(i + 1) * w], in_=prep_src(p)[:, i * w:(i + 1) * w])
             xin[p] = t
 
-        def load_b(q, cuts):
-            t = bpool.tile([P, 2048], BF16, name="bsb%d" % q, tag="bsb")
-            tv = t[:].rearrange("p (G r) -> p G r", G=4)
-            for lo, hi in cuts:
-                nc.sync.dma_start(out=tv[:, lo:hi, :], in_=bv[q][:, lo:hi, :])
-            bsb[q] = t
+        def load_b(lo, hi):
+            q = lo // 4
+            if q not in bsb:
+                bsb[q] = bpool.tile([P, 2048], BF16, name="bsb%d" % q, tag="bsb")
+            tv = bsb[q][:].rearrange("p (G r) -> p G r", G=4)
+            nc.sync.dma_start(out=tv[:, lo - 4 * q:hi - 4 * q, :], in_=bv[q][:, lo - 4 * q:hi - 4 * q, :])
 
-        def prep_t(p):
+        def transposes(p):
             xf = xin[p][:].bitcast(F32)
-            gt = grpool.tile([P, 2048], BF16, name="grp%d" % p, tag="grp", align_bytes=64)
-            grp[p] = gt
-            gf = gt[:].bitcast(F32).rearrange("p (c u) -> p c u", u=2)
             for bb in range(2):
                 xt = psb.tile([P, 512], F32, name="xt%d_%d" % (p, bb), tag="bank")
+                xts[p, bb] = xt
                 for aa in range(2):
                     for u2 in range(2):
                         a = 2 * bb + aa
@@ -110,16 +91,17 @@ def tile_routing_t_kernel(tc, x, W, b, out):
                             xf[:, a * 256 + u2 * P: a * 256 + u2 * P + P],
                             ident[:],
                         )
-                if bb == 1 and p % TE_ACT_EVERY == TE_ACT_EVERY - 1:
-                    nc.scalar.copy(
-                        out=gf[:, bb * 256:(bb + 1) * 256, :],
-                        in_=xt[:].rearrange("p (u c) -> p c u", u=2),
-                    )
-                else:
-                    nc.vector.tensor_copy(
-                        out=gf[:, bb * 256:(bb + 1) * 256, :],
-                        in_=xt[:].rearrange("p (u c) -> p c u", u=2),
-                    )
+
+        def evac_t(p, bb, eng="v"):
+            if p not in grp:
+                grp[p] = grpool.tile([P, 2048], BF16, name="grp%d" % p, tag="grp", align_bytes=64)
+            gf = grp[p][:].bitcast(F32).rearrange("p (c u) -> p c u", u=2)
+            dst = gf[:, bb * 256:(bb + 1) * 256, :]
+            src = xts[p, bb][:].rearrange("p (u c) -> p c u", u=2)
+            if eng == "a":
+                nc.scalar.copy(out=dst, in_=src)
+            else:
+                nc.vector.tensor_copy(out=dst, in_=src)
 
         def q1(p):
             ct = copool.tile([P, 512], U32, name="cod%d" % p, tag="cod", align_bytes=64)
@@ -131,55 +113,48 @@ def tile_routing_t_kernel(tc, x, W, b, out):
         def slot_ops(s):
             g, r = divmod(s, 4)
             au, aw = ((0, 0), (0, 1), (1, 1), (1, 0))[r]
-            pu = 4 * g + (0, 3)[au]
-            pw = 4 * g + (1, 2)[aw]
-            return g, au, aw, pu, pw
+            return g, au, aw, 4 * g + (0, 3)[au], 4 * g + (1, 2)[aw]
 
-        def mx1(s, evac):
+        def mx1(s, nq):
             g, au, aw, pu, pw = slot_ops(s)
-            pg = pgpool.tile([P, 2048], BF16, name="pg%d" % s, tag="pg", align_bytes=64)
-            pgt[s] = pg
-            for nq in range(4):
-                pp = psb.tile([P, 512], F32, name="pp%d_%d" % (s, nq), tag="bank")
-                for j in range(4):
-                    nc.tensor.matmul_mx(
-                        out=(pp[:].rearrange("p (n j) -> p j n", j=4)[:, j, :] if STRIDED_OUT else pp[:, j * P:(j + 1) * P]),
-                        lhsT=cod[pu][:, j * P:(j + 1) * P].bitcast(FP8X4),
-                        lhsT_scale=pln[pu][:, j * P:(j + 1) * P],
-                        rhs=cod[pw][:, nq * P:(nq + 1) * P].bitcast(FP8X4),
-                        rhs_scale=pln[pw][:, nq * P:(nq + 1) * P],
-                        start=True,
-                        stop=True,
-                    )
-                if STRIDED_OUT:
-                    dst = pg[:, nq * 512:(nq + 1) * 512]
-                    src = pp[:]
-                else:
-                    dst = pg[:, nq * 512:(nq + 1) * 512].rearrange("p (n j) -> p n j", j=4)
-                    src = pp[:].rearrange("p (j n) -> p n j", j=4)
-                if PE_ANY:
-                    nc.any.tensor_copy(out=dst, in_=src)
-                elif evac[nq] == "a":
-                    nc.scalar.copy(out=dst, in_=src)
-                else:
-                    nc.vector.tensor_copy(out=dst, in_=src)
+            pp = psb.tile([P, 512], F32, name="pp%d_%d" % (s, nq), tag="bank")
+            for j in range(4):
+                nc.tensor.matmul_mx(
+                    out=pp[:, j * P:(j + 1) * P],
+                    lhsT=cod[pu][:, j * P:(j + 1) * P].bitcast(FP8X4),
+                    lhsT_scale=pln[pu][:, j * P:(j + 1) * P],
+                    rhs=cod[pw][:, nq * P:(nq + 1) * P].bitcast(FP8X4),
+                    rhs_scale=pln[pw][:, nq * P:(nq + 1) * P],
+                    start=True,
+                    stop=True,
+                )
+            xts[s, nq, "p"] = pp
 
-        def q2(s):
-            ct = pcpool.tile([P, 512], U32, name="pcd%d" % s, tag="pcd", align_bytes=64)
-            pt = pcpool.tile([P, 512], U8, name="ppl%d" % s, tag="ppl", align_bytes=64)
-            nc.vector.quantize_mx(out=ct[:].bitcast(FP8X4), scales=pt[:], in_=pgt[s][:])
-            pcd[s] = ct
-            ppl[s] = pt
+        def evac_p(s, nq, eng="a"):
+            if s not in pgt:
+                pgt[s] = pgpool.tile([P, 2048], BF16, name="pg%d" % s, tag="pg", align_bytes=64)
+            dst = pgt[s][:, nq * 512:(nq + 1) * 512].rearrange("p (n j) -> p n j", j=4)
+            src = xts[s, nq, "p"][:].rearrange("p (j n) -> p n j", j=4)
+            if eng == "a":
+                nc.scalar.copy(out=dst, in_=src)
+            else:
+                nc.vector.tensor_copy(out=dst, in_=src)
 
-        def mx2(s):
+        def q2(s, lo=0, hi=512):
+            if s not in pcd:
+                pcd[s] = pcpool.tile([P, 512], U32, name="pcd%d" % s, tag="pcd", align_bytes=64)
+                ppl[s] = pcpool.tile([P, 512], U8, name="ppl%d" % s, tag="ppl", align_bytes=64)
+            nc.vector.quantize_mx(out=pcd[s][:, lo:hi].bitcast(FP8X4), scales=ppl[s][:, lo:hi], in_=pgt[s][:, 4 * lo:4 * hi])
+
+        def mx2(s, lo=0, hi=512):
             g, au, aw, pu, pw = slot_ops(s)
             un = 2 * g + au
             nc.tensor.matmul_mx(
-                out=s_acc[aw][:],
+                out=s_acc[aw][:, lo:hi],
                 lhsT=ccodes[:, un * P:(un + 1) * P].bitcast(FP8X4),
                 lhsT_scale=cplane[:, un * P:(un + 1) * P],
-                rhs=pcd[s][:].bitcast(FP8X4),
-                rhs_scale=ppl[s][:],
+                rhs=pcd[s][:, lo:hi].bitcast(FP8X4),
+                rhs_scale=ppl[s][:, lo:hi],
                 start=(un == 0),
                 stop=(un == NUNIT - 1),
             )
@@ -188,54 +163,53 @@ def tile_routing_t_kernel(tc, x, W, b, out):
             q, gl = divmod(un, 4)
             return bsb[q][:, gl * 512:(gl + 1) * 512]
 
-        def sm_tiles(un):
-            sums[un] = small.tile([P, 4], F32, name="sums%d" % un, tag="sums")
-            etl[un] = epool.tile([P, 512], F32, name="etl%d" % un, tag="etl")
-
-        def sm_max(un):
-            nm = small.tile([P, 4], F32, name="nmx%d" % un, tag="nmx")
+        def max_unit(un):
             nc.vector.tensor_reduce(
-                out=nm[:], in_=b_unit(un).rearrange("p (r o) -> p r o", o=NO),
+                out=nmx[:, 4 * un:4 * un + 4], in_=b_unit(un).rearrange("p (r o) -> p r o", o=NO),
                 axis=AX.X, op=ALU.max, negate=True,
             )
-            nmx[un] = nm[:]
-            sm_tiles(un)
 
-        def sm_max_chunk(q, lo=0):
-            nr = 4 * (4 - lo)
-            bs = bsb[q][:, lo * 512:2048].rearrange("p (r o) -> p r o", o=NO)
-            m1 = mpool.tile([P, 16, 64], BF16, name="m1_%d" % q, tag="m1")
-            m2 = mpool.tile([P, 16, 32], BF16, name="m2_%d" % q, tag="m2")
-            m3 = mpool.tile([P, 16, 16], BF16, name="m3_%d" % q, tag="m3")
-            nm = small.tile([P, 16], F32, name="nmc%d" % q, tag="nmc", bufs=3)
-            nc.vector.tensor_tensor(out=m1[:, 0:nr, :], in0=bs[:, :, 0:64], in1=bs[:, :, 64:128], op=ALU.max)
-            nc.vector.tensor_tensor(out=m2[:, 0:nr, :], in0=m1[:, 0:nr, 0:32], in1=m1[:, 0:nr, 32:64], op=ALU.max)
-            nc.vector.tensor_tensor(out=m3[:, 0:nr, :], in0=m2[:, 0:nr, 0:16], in1=m2[:, 0:nr, 16:32], op=ALU.max)
-            nc.vector.tensor_reduce(out=nm[:, 0:nr], in_=m3[:, 0:nr, :], axis=AX.X, op=ALU.max, negate=True)
-            for gl in range(lo, 4):
-                nmx[4 * q + gl] = nm[:, 4 * (gl - lo):4 * (gl - lo) + 4]
+        def max_level(lo, hi, level):
+            q = lo // 4
+            nr = 4 * (hi - lo)
+            if level == 0:
+                src = bsb[q][:, (lo - 4 * q) * 512:(hi - 4 * q) * 512].rearrange("p (r o) -> p r o", o=NO)
+            else:
+                src = tree[lo, level - 1][:, 0:nr, :]
+            w = NO >> (level + 1)
+            if level == 4:
+                nc.vector.tensor_reduce(out=nmx[:, 4 * lo:4 * hi], in_=src, axis=AX.X, op=ALU.max, negate=True)
+            else:
+                m = mpool.tile([P, 16, w], BF16, name="m%d_%d" % (level, lo), tag="m%d" % level)
+                nc.vector.tensor_tensor(out=m[:, 0:nr, :], in0=src[:, :, 0:w], in1=src[:, :, w:2 * w], op=ALU.max)
+                tree[lo, level] = m
 
-        def sm_exp(un, j):
-            if un not in etl:
-                sm_tiles(un)
+        def sm_exp(e):
+            un, j = divmod(e, 4)
+            if j == 0:
+                etl[un] = epool.tile([P, 512], F32, name="etl%d" % un, tag="etl")
+                if un % 2 == 0:
+                    sums[un // 2] = small.tile([P, 8], F32, name="sums%d" % un, tag="sums")
+            k = 4 * (un % 2) + j
             nc.scalar.activation(
                 out=etl[un][:, j * NO:(j + 1) * NO], in_=b_unit(un)[:, j * NO:(j + 1) * NO],
-                func=ACTF.Exp, bias=nmx[un][:, j:j + 1], scale=1.0,
-                accum_out=sums[un][:, j:j + 1],
+                func=ACTF.Exp, bias=nmx[:, e:e + 1], scale=1.0,
+                accum_out=sums[un // 2][:, k:k + 1],
             )
 
-        def sm_rec(un):
-            rs = small.tile([P, 4], F32, name="rs%d" % un, tag="rs")
-            nc.vector.reciprocal(out=rs[:], in_=sums[un][:])
-            rcp[un] = rs
+        def sm_rec(g):
+            rs = small.tile([P, 8], F32, name="rs%d" % g, tag="rs")
+            nc.vector.reciprocal(out=rs[:], in_=sums[g][:])
+            rcp[g] = rs
 
         def sm_half(k):
             un, h = divmod(k, 2)
+            g, u = divmod(un, 2)
             cg = cgpool.tile([P, 256], BF16, name="cg%d" % k, tag="cg", align_bytes=64)
             nc.gpsimd.tensor_tensor(
                 out=cg[:].rearrange("p (o j) -> p o j", j=4),
                 in0=etl[un][:].rearrange("p (j o) -> p o j", j=4)[:, h * 64:(h + 1) * 64, :],
-                in1=rcp[un][:].unsqueeze(1).to_broadcast([P, 64, 4]),
+                in1=rcp[g][:, 4 * u:4 * u + 4].unsqueeze(1).to_broadcast([P, 64, 4]),
                 op=ALU.mult,
             )
             cgt[k] = cg
@@ -247,85 +221,113 @@ def tile_routing_t_kernel(tc, x, W, b, out):
                 in_=cgt[k][:],
             )
 
-        dve_fill = {}
-        act_fill = {}
-
-        def add(d, t, item):
-            if t not in d:
-                d[t] = []
-            d[t].append(item)
-
-        for un in range(HEAD_UNITS, NUNIT):
-            first = 4 * (un - HEAD_UNITS)
-            if un % 4 == 0:
-                add(dve_fill, EXP_T0 + (first * EXP_NUM) // 16 - 2, ("maxc", un // 4))
-            for j in range(4):
-                add(act_fill, EXP_T0 + ((first + j) * EXP_NUM) // 16, (un, j))
+        n2 = [const.tile([P, 1], F32, name="n2_%d" % a) for a in range(2)]
+        n1e = const.tile([P, 1], F32, name="n1e")
 
         nc.vector.memset(dum[:], 1.0)
         nc.scalar.activation(out=dum2[:], in_=dum[:], func=ACTF.Exp)
         make_identity(nc, ident[:])
-        load_b(0, ((0, 1), (1, 4)))
-        load_b(1, ((0, 4),))
-        for p in range(4):
+        load_b(0, 1)
+        load_b(1, 2)
+        load(0, 2)
+        load(1, 2)
+        load_b(2, 4)
+        load(2)
+        load(3)
+        load_b(4, 8)
+        load(4)
+        load(5)
+        load(6)
+        load_b(8, 12)
+        load(7)
+        load(8)
+        load(9)
+        load_b(12, 16)
+        for p in range(10, NB):
             load(p)
-        load_b(2, ((0, 4),))
-        for p in range(4, 8):
-            load(p)
-        load_b(3, ((0, 4),))
-        for p in range(8, NB):
-            load(p)
-        sm_max(0)
-        for j in range(4):
-            sm_exp(0, j)
-        sm_max_chunk(0, 1)
-        for un in range(1, 4):
-            for j in range(4):
-                sm_exp(un, j)
-        sm_max_chunk(1)
-        for un in range(4, HEAD_UNITS):
-            for j in range(4):
-                sm_exp(un, j)
+        max_unit(0)
+        max_unit(1)
+        for e in range(4):
+            sm_exp(e)
+        transposes(0)
+        transposes(1)
+        evac_t(0, 0)
+        evac_t(0, 1, "a")
+        evac_t(1, 0)
+        evac_t(1, 1, "a")
+        for e in range(4, 8):
+            sm_exp(e)
+        transposes(2)
+        q1(0)
+        max_level(2, 4, 0)
+        q1(1)
+        max_level(2, 4, 1)
+        evac_t(2, 0)
+        max_level(2, 4, 2)
+        evac_t(2, 1)
+        max_level(2, 4, 3)
+        max_level(2, 4, 4)
+        sm_rec(0)
+        sm_half(0)
+        done = 8
+        MAXQ = {}
+        for i, t0 in ((1, 1), (2, 9), (3, 17)):
+            for l in range(5):
+                MAXQ[t0 * 3 + l] = (4 * i, 4 * i + 4, l)
 
-        n2 = [const.tile([P, 1], F32, name="n2_%d" % a) for a in range(2)]
-        n1e = const.tile([P, 1], F32, name="n1e")
+        def tree_piece(n):
+            if n in MAXQ:
+                max_level(*MAXQ[n])
 
-        for t in range(-3, NSLOT + M2LAG):
-            if t == -3:
-                sm_rec(0)
-            if t < 0 and 0 <= t + 2:
-                q1(t + 2)
-            if 0 <= t + 3 < NPREP:
-                prep_t(t + 3)
-                if t + 3 + NB < NPREP:
-                    load(t + 3 + NB)
+        for t in range(0, NSLOT + M2LAG):
+            k = t + 1
+            if t + 3 < NPREP:
+                transposes(t + 3)
+                if t + NB < NPREP:
+                    load(t + NB)
             if 0 <= t - M2LAG < NSLOT:
                 mx2(t - M2LAG)
-                if t - M2LAG == NSLOT - 2:
-                    nc.scalar.activation(out=junk[:], in_=s_acc[1][:], func=ACTF.Square, accum_out=n2[1][:])
-                    nc.vector.tensor_scalar(out=n1e[:], in0=n2[1][:], scalar1=EPS, scalar2=None, op0=ALU.add)
-            for un, j in act_fill.get(t, []):
-                sm_exp(un, j)
-            late = t >= TAIL_T
-            for when in (True, False):
-                if late == when:
-                    if t >= 0 and t + 2 < NPREP:
-                        q1(t + 2)
-                    for kind, un in dve_fill.get(t, []):
-                        sm_max_chunk(un)
-                    k = t + 3
-                    if 0 <= k - 1 < 2 * NUNIT:
-                        sm_qh(k - 1)
-                    if k % 2 == 1 and (k + 1) // 2 < NUNIT:
-                        sm_rec((k + 1) // 2)
-                    if k < 2 * NUNIT:
-                        sm_half(k)
-                    if 0 <= t - 1 < NSLOT:
-                        q2(t - 1)
-                if when and 0 <= t < NSLOT:
-                    mx1(t, "avav" if late else "aaaa")
-                    if t == NSLOT - 1:
-                        nc.scalar.activation(out=dum2[:], in_=dum[:], func=ACTF.Sqrt)
+            if t < NSLOT:
+                for nq in range(4):
+                    mx1(t, nq)
+            upto = min(64, 12 + 2 * t)
+            for e in range(done, upto):
+                sm_exp(e)
+            done = max(done, upto)
+            if t < NSLOT:
+                for nq in range(4):
+                    if ("avav"[nq] if t >= 30 else "a") == "a":
+                        evac_p(t, nq)
+            if t + 3 < NPREP:
+                evac_t(t + 3, 0)
+            tree_piece(3 * t)
+            if t + 3 < NPREP:
+                evac_t(t + 3, 1)
+            tree_piece(3 * t + 1)
+            if t < NSLOT:
+                for nq in range(2):
+                    if ("avav"[nq] if t >= 30 else "a") == "v":
+                        evac_p(t, nq, "v")
+            if t + 2 < NPREP:
+                q1(t + 2)
+            if t < 2 * NUNIT:
+                sm_qh(t)
+            if k % 4 == 0 and k // 4 < NS:
+                sm_rec(k // 4)
+            tree_piece(3 * t + 2)
+            if k < 2 * NUNIT:
+                sm_half(k)
+            if 0 <= t - 1 < NSLOT:
+                q2(t - 1)
+            if t < NSLOT:
+                for nq in range(2, 4):
+                    if ("avav"[nq] if t >= 30 else "a") == "v":
+                        evac_p(t, nq, "v")
+            if t == NSLOT - 1:
+                nc.scalar.activation(out=dum2[:], in_=dum[:], func=ACTF.Sqrt)
+            if t - M2LAG == NSLOT - 2:
+                nc.scalar.activation(out=junk[:], in_=s_acc[1][:], func=ACTF.Square, accum_out=n2[1][:])
+                nc.vector.tensor_scalar(out=n1e[:], in0=n2[1][:], scalar1=EPS, scalar2=None, op0=ALU.add)
 
         nc.scalar.activation(out=junk[:], in_=s_acc[0][:], func=ACTF.Square, accum_out=n2[0][:])
         rt = const.tile([P, 1], F32, name="rt")

@@ -223,6 +223,7 @@ def tile_routing_t_kernel(tc, x, W, b, out):
 
         n2 = [const.tile([P, 1], F32, name="n2_%d" % a) for a in range(2)]
         n1e = const.tile([P, 1], F32, name="n1e")
+        n1p = const.tile([P, 1], F32, name="n1p")
 
         nc.vector.memset(dum[:], 1.0)
         nc.scalar.activation(out=dum2[:], in_=dum[:], func=ACTF.Exp)
@@ -262,9 +263,9 @@ def tile_routing_t_kernel(tc, x, W, b, out):
         max_level(2, 4, 0)
         q1(1)
         max_level(2, 4, 1)
-        evac_t(2, 0)
+        evac_t(2, 0, "a")
         max_level(2, 4, 2)
-        evac_t(2, 1)
+        evac_t(2, 1, "a")
         max_level(2, 4, 3)
         max_level(2, 4, 4)
         sm_rec(0)
@@ -296,7 +297,7 @@ def tile_routing_t_kernel(tc, x, W, b, out):
             done = max(done, upto)
             if t < NSLOT:
                 for nq in range(4):
-                    if ("avav"[nq] if t >= 30 else "a") == "a":
+                    if ("avav"[nq] if t == NSLOT - 1 else "aava"[nq] if t >= NSLOT - 3 else "a") == "a":
                         evac_p(t, nq)
             if t + 3 < NPREP:
                 evac_t(t + 3, 0)
@@ -306,7 +307,7 @@ def tile_routing_t_kernel(tc, x, W, b, out):
             tree_piece(3 * t + 1)
             if t < NSLOT:
                 for nq in range(2):
-                    if ("avav"[nq] if t >= 30 else "a") == "v":
+                    if ("avav"[nq] if t == NSLOT - 1 else "aava"[nq] if t >= NSLOT - 3 else "a") == "v":
                         evac_p(t, nq, "v")
             if t + 2 < NPREP:
                 q1(t + 2)
@@ -321,29 +322,26 @@ def tile_routing_t_kernel(tc, x, W, b, out):
                 q2(t - 1)
             if t < NSLOT:
                 for nq in range(2, 4):
-                    if ("avav"[nq] if t >= 30 else "a") == "v":
+                    if ("avav"[nq] if t == NSLOT - 1 else "aava"[nq] if t >= NSLOT - 3 else "a") == "v":
                         evac_p(t, nq, "v")
             if t == NSLOT - 1:
-                nc.scalar.activation(out=dum2[:], in_=dum[:], func=ACTF.Sqrt)
+                nc.scalar.activation(out=dum2[:], in_=dum[:], func=ACTF.Abs_reciprocal_sqrt)
             if t - M2LAG == NSLOT - 2:
                 nc.scalar.activation(out=junk[:], in_=s_acc[1][:], func=ACTF.Square, accum_out=n2[1][:])
                 nc.vector.tensor_scalar(out=n1e[:], in0=n2[1][:], scalar1=EPS, scalar2=None, op0=ALU.add)
+                nc.vector.tensor_scalar(out=n1p[:], in0=n2[1][:], scalar1=1.0, scalar2=None, op0=ALU.add)
 
         nc.scalar.activation(out=junk[:], in_=s_acc[0][:], func=ACTF.Square, accum_out=n2[0][:])
-        rt = const.tile([P, 1], F32, name="rt")
-        n2s = const.tile([P, 1], F32, name="n2s")
+        rr = const.tile([P, 1], F32, name="rr")
         den = const.tile([P, 1], F32, name="den")
         rden = const.tile([P, 1], F32, name="rden")
         mfac = const.tile([P, 1], F32, name="mfac")
-        rrt = const.tile([P, 1], F32, name="rrt")
         fac = const.tile([P, 1], F32, name="fac")
-        nc.scalar.activation(out=rt[:], in_=n2[0][:], func=ACTF.Sqrt, bias=n1e[:, 0:1], scale=1.0)
-        nc.vector.tensor_tensor(out=n2s[:], in0=n2[0][:], in1=n2[1][:], op=ALU.add)
-        nc.vector.tensor_scalar(out=den[:], in0=n2s[:], scalar1=1.0, scalar2=None, op0=ALU.add)
+        nc.scalar.activation(out=rr[:], in_=n2[0][:], func=ACTF.Abs_reciprocal_sqrt, bias=n1e[:, 0:1], scale=1.0)
+        nc.vector.tensor_tensor(out=den[:], in0=n2[0][:], in1=n1p[:], op=ALU.add)
         nc.vector.reciprocal(out=rden[:], in_=den[:])
-        nc.vector.tensor_tensor(out=mfac[:], in0=n2s[:], in1=rden[:], op=ALU.mult)
-        nc.vector.reciprocal(out=rrt[:], in_=rt[:])
-        nc.vector.tensor_tensor(out=fac[:], in0=mfac[:], in1=rrt[:], op=ALU.mult)
+        nc.vector.scalar_tensor_tensor(out=mfac[:], in0=n2[0][:], scalar=n2[1][:, 0:1], in1=rden[:], op0=ALU.add, op1=ALU.mult)
+        nc.scalar.activation(out=fac[:], in_=mfac[:], func=ACTF.Copy, scale=rr[:, 0:1])
         for h in range(2):
             for a in (1, 0):
                 lo = a * 512 + h * 256
@@ -352,5 +350,5 @@ def tile_routing_t_kernel(tc, x, W, b, out):
                 if a == 0:
                     nc.scalar.activation(out=dst, in_=src, func=ACTF.Copy, scale=fac[:, 0:1])
                 else:
-                    nc.vector.tensor_scalar(out=dst, in0=src, scalar1=fac[:, 0:1], scalar2=None, op0=ALU.mult)
+                    nc.vector.tensor_scalar(out=dst, in0=src, scalar1=mfac[:, 0:1], scalar2=rr[:, 0:1], op0=ALU.mult, op1=ALU.mult)
                 nc.sync.dma_start(out=out[:, lo:lo + 256], in_=out_sb[:, lo:lo + 256])

@@ -207,9 +207,9 @@ def tile_routing_t_kernel(tc, x, W, b, out):
             g, u = divmod(un, 2)
             cg = cgpool.tile([P, 256], BF16, name="cg%d" % k, tag="cg", align_bytes=64)
             nc.gpsimd.tensor_tensor(
-                out=cg[:].rearrange("p (o j) -> p o j", j=4),
-                in0=etl[un][:].rearrange("p (j o) -> p o j", j=4)[:, h * 64:(h + 1) * 64, :],
-                in1=rcp[g][:, 4 * u:4 * u + 4].unsqueeze(1).to_broadcast([P, 64, 4]),
+                out=cg[:].rearrange("p (c i j) -> p c j i", i=4, j=4),
+                in0=etl[un][:].rearrange("p (j c i) -> p c j i", j=4, i=4)[:, h * 16:(h + 1) * 16, :, :],
+                in1=rcp[g][:, 4 * u:4 * u + 4].unsqueeze(1).unsqueeze(3).to_broadcast([P, 16, 4, 4]),
                 op=ALU.mult,
             )
             cgt[k] = cg

@@ -224,8 +224,10 @@ def tile_routing_t_kernel(tc, x, W, b, out):
         n2 = [const.tile([P, 1], F32, name="n2_%d" % a) for a in range(2)]
         n1e = const.tile([P, 1], F32, name="n1e")
         n1p = const.tile([P, 1], F32, name="n1p")
+        mhalf = const.tile([P, 1], F32, name="mhalf")
 
         nc.vector.memset(dum[:], 1.0)
+        nc.vector.memset(mhalf[:], -0.5)
         nc.scalar.activation(out=dum2[:], in_=dum[:], func=ACTF.Exp)
         make_identity(nc, ident[:])
         load_b(0, 1)
@@ -272,9 +274,9 @@ def tile_routing_t_kernel(tc, x, W, b, out):
         sm_half(0)
         done = 8
         MAXQ = {}
-        for i, t0 in ((1, 1), (2, 9), (3, 17)):
+        for i, t0 in ((1, 0), (2, 8), (3, 16)):
             for l in range(5):
-                MAXQ[t0 * 3 + l] = (4 * i, 4 * i + 4, l)
+                MAXQ[t0 * 2 + l] = (4 * i, 4 * i + 4, l)
 
         def tree_piece(n):
             if n in MAXQ:
@@ -297,35 +299,31 @@ def tile_routing_t_kernel(tc, x, W, b, out):
             done = max(done, upto)
             if t < NSLOT:
                 for nq in range(4):
-                    if ("avav"[nq] if t == NSLOT - 1 else "aava"[nq] if t >= NSLOT - 3 else "a") == "a":
+                    if {28: "aaav", 29: "aaav", 31: "avva"}.get(t, "aaaa")[nq] == "a":
                         evac_p(t, nq)
             if t + 3 < NPREP:
                 evac_t(t + 3, 0)
-            tree_piece(3 * t)
-            if t + 3 < NPREP:
                 evac_t(t + 3, 1)
-            tree_piece(3 * t + 1)
-            if t < NSLOT:
-                for nq in range(2):
-                    if ("avav"[nq] if t == NSLOT - 1 else "aava"[nq] if t >= NSLOT - 3 else "a") == "v":
-                        evac_p(t, nq, "v")
+            tree_piece(2 * t)
+            if t == NSLOT - 1:
+                evac_p(t, 1, "v")
             if t + 2 < NPREP:
                 q1(t + 2)
+            tree_piece(2 * t + 1)
             if t < 2 * NUNIT:
                 sm_qh(t)
             if k % 4 == 0 and k // 4 < NS:
                 sm_rec(k // 4)
-            tree_piece(3 * t + 2)
             if k < 2 * NUNIT:
                 sm_half(k)
-            if 0 <= t - 1 < NSLOT:
+            if 0 <= t - 1 < NSLOT - 1:
                 q2(t - 1)
             if t < NSLOT:
-                for nq in range(2, 4):
-                    if ("avav"[nq] if t == NSLOT - 1 else "aava"[nq] if t >= NSLOT - 3 else "a") == "v":
+                for nq in range(4):
+                    if {28: "aaav", 29: "aaav", 31: "avva"}.get(t, "aaaa")[nq] == "v" and (t, nq) != (NSLOT - 1, 1):
                         evac_p(t, nq, "v")
             if t == NSLOT - 1:
-                nc.scalar.activation(out=dum2[:], in_=dum[:], func=ACTF.Abs_reciprocal_sqrt)
+                q2(t)
             if t - M2LAG == NSLOT - 2:
                 nc.scalar.activation(out=junk[:], in_=s_acc[1][:], func=ACTF.Square, accum_out=n2[1][:])
                 nc.vector.tensor_scalar(out=n1e[:], in0=n2[1][:], scalar1=EPS, scalar2=None, op0=ALU.add)
@@ -333,11 +331,13 @@ def tile_routing_t_kernel(tc, x, W, b, out):
 
         nc.scalar.activation(out=junk[:], in_=s_acc[0][:], func=ACTF.Square, accum_out=n2[0][:])
         rr = const.tile([P, 1], F32, name="rr")
+        n2e = const.tile([P, 1], F32, name="n2e")
         den = const.tile([P, 1], F32, name="den")
         rden = const.tile([P, 1], F32, name="rden")
         mfac = const.tile([P, 1], F32, name="mfac")
         fac = const.tile([P, 1], F32, name="fac")
-        nc.scalar.activation(out=rr[:], in_=n2[0][:], func=ACTF.Abs_reciprocal_sqrt, bias=n1e[:, 0:1], scale=1.0)
+        nc.gpsimd.tensor_tensor(out=n2e[:], in0=n2[0][:], in1=n1e[:], op=ALU.add)
+        nc.gpsimd.tensor_tensor(out=rr[:], in0=n2e[:], in1=mhalf[:], op=ALU.pow)
         nc.vector.tensor_tensor(out=den[:], in0=n2[0][:], in1=n1p[:], op=ALU.add)
         nc.vector.reciprocal(out=rden[:], in_=den[:])
         nc.vector.scalar_tensor_tensor(out=mfac[:], in0=n2[0][:], scalar=n2[1][:, 0:1], in1=rden[:], op0=ALU.add, op1=ALU.mult)

@@ -156,7 +156,7 @@ def tile_routing_t_kernel(tc, x, W, b, out):
                 rhs=pcd[s][:, lo:hi].bitcast(FP8X4),
                 rhs_scale=ppl[s][:, lo:hi],
                 start=(un == 0),
-                stop=(un == NUNIT - 1),
+                stop=(un == NUNIT - 1 and hi == 512),
             )
 
         def b_unit(un):
@@ -288,8 +288,11 @@ def tile_routing_t_kernel(tc, x, W, b, out):
                 transposes(t + 3)
                 if t + NB < NPREP:
                     load(t + NB)
-            if 0 <= t - M2LAG < NSLOT:
+            if 0 <= t - M2LAG < NSLOT - 1:
                 mx2(t - M2LAG)
+            if t - M2LAG == NSLOT - 1:
+                mx2(NSLOT - 1, 0, 256)
+                mx2(NSLOT - 1, 256, 512)
             if t < NSLOT:
                 for nq in range(4):
                     mx1(t, nq)
@@ -299,7 +302,7 @@ def tile_routing_t_kernel(tc, x, W, b, out):
             done = max(done, upto)
             if t < NSLOT:
                 for nq in range(4):
-                    if {28: "aaav", 29: "aaav", 31: "avva"}.get(t, "aaaa")[nq] == "a":
+                    if ("avaa"[nq] if t == NSLOT - 1 else "aaav"[nq] if t >= NSLOT - 4 else "a") == "a":
                         evac_p(t, nq)
             if t + 3 < NPREP:
                 evac_t(t + 3, 0)
@@ -320,10 +323,11 @@ def tile_routing_t_kernel(tc, x, W, b, out):
                 q2(t - 1)
             if t < NSLOT:
                 for nq in range(4):
-                    if {28: "aaav", 29: "aaav", 31: "avva"}.get(t, "aaaa")[nq] == "v" and (t, nq) != (NSLOT - 1, 1):
+                    if ("avaa"[nq] if t == NSLOT - 1 else "aaav"[nq] if t >= NSLOT - 4 else "a") == "v" and (t, nq) != (NSLOT - 1, 1):
                         evac_p(t, nq, "v")
             if t == NSLOT - 1:
-                q2(t)
+                q2(t, 0, 256)
+                q2(t, 256, 512)
             if t - M2LAG == NSLOT - 2:
                 nc.scalar.activation(out=junk[:], in_=s_acc[1][:], func=ACTF.Square, accum_out=n2[1][:])
                 nc.vector.tensor_scalar(out=n1e[:], in0=n2[1][:], scalar1=EPS, scalar2=None, op0=ALU.add)

from contextlib import ExitStack

import concourse.mybir as mybir
from concourse.masks import make_identity

F32 = mybir.dt.float32
BF16 = mybir.dt.bfloat16
U32 = mybir.dt.uint32
U8 = mybir.dt.uint8
FP8X4 = mybir.dt.float8_e4m3fn_x4
ACTF = mybir.ActivationFunctionType
ALU = mybir.AluOpType
AX = mybir.AxisListType

P = 128
NS, HW, DI, DO, NO = 8, 1024, 512, 1024, 128
NIN = NS * HW
EPS = 1e-8
FLOPS = 2 * NS * HW * DO * DI + 2 * NIN * NO * DO

NB = 16
NPREP = 32
NSLOT = 32
NUNIT = 16
M2LAG = 3


def tile_routing_t_kernel(tc, x, W, b, out):
    nc = tc.nc
    xv = x.rearrange("o c h w -> (o c h w)").rearrange("(g A p r) -> g A p r", g=NS, A=2, p=P)
    wv = W.rearrange("g (A p a) f -> g A p (a f)", A=2, p=P)
    bv = b.rearrange("(q G p j) o -> q p G (j o)", q=4, G=4, p=P)

    with ExitStack() as ctx:
        const = ctx.enter_context(tc.tile_pool(name="const", bufs=1))
        inpool = ctx.enter_context(tc.tile_pool(name="inpool", bufs=NB))
        bpool = ctx.enter_context(tc.tile_pool(name="bpool", bufs=4))
        epool = ctx.enter_context(tc.tile_pool(name="epool", bufs=8))
        small = ctx.enter_context(tc.tile_pool(name="small", bufs=4))
        mpool = ctx.enter_context(tc.tile_pool(name="mpool", bufs=1))
        cgpool = ctx.enter_context(tc.tile_pool(name="cgpool", bufs=1))
        grpool = ctx.enter_context(tc.tile_pool(name="grpool", bufs=3))
        copool = ctx.enter_context(tc.tile_pool(name="copool", bufs=8))
        pgpool = ctx.enter_context(tc.tile_pool(name="pgpool", bufs=3))
        pcpool = ctx.enter_context(tc.tile_pool(name="pcpool", bufs=5))
        psacc = ctx.enter_context(tc.psum_pool(name="psacc", bufs=1))
        psb = ctx.enter_context(tc.psum_pool(name="psb", bufs=6))
        ctx.enter_context(tc.manual_schedule())

        ident = const.tile([P, P], F32, name="ident")
        ccodes = const.tile([P, NUNIT * P], U32, name="ccodes", align_bytes=64)
        cplane = const.tile([P, NUNIT * P], U8, name="cplane", align_bytes=64)
        out_sb = const.tile([P, DO], F32, name="out_sb")
        junk = const.tile([P, 512], F32, name="junk")
        dum = const.tile([P, 1], F32, name="dum")
        dum2 = const.tile([P, 1], F32, name="dum2")
        nmx = const.tile([P, 4 * NUNIT], F32, name="nmx")
        s_acc = [psacc.tile([P, 512], F32, name="s_acc%d" % a) for a in range(2)]

        xin, grp, cod, pln, pgt, pcd, ppl, bsb = {}, {}, {}, {}, {}, {}, {}, {}
        sums, etl, cgt, rcp, tree, xts = {}, {}, {}, {}, {}, {}

        def prep_src(p):
            g, r = divmod(p, 4)
            return (xv[g, 0], wv[g, 0], wv[g, 1], xv[g, 1])[r]

        def load(p, parts=1):
            t = inpool.tile([P, 2048], BF16, name="xin%d" % p, tag="xin")
            w = 2048 // parts
            for i in range(parts):
                nc.sync.dma_start(out=t[:, i * w:(i + 1) * w], in_=prep_src(p)[:, i * w:(i + 1) * w])
            xin[p] = t

        def load_b(lo, hi):
            q = lo // 4
            if q not in bsb:
                bsb[q] = bpool.tile([P, 2048], BF16, name="bsb%d" % q, tag="bsb")
            tv = bsb[q][:].rearrange("p (G r) -> p G r", G=4)
            nc.sync.dma_start(out=tv[:, lo - 4 * q:hi - 4 * q, :], in_=bv[q][:, lo - 4 * q:hi - 4 * q, :])

        def transposes(p):
            xf = xin[p][:].bitcast(F32)
            for bb in range(2):
                xt = psb.tile([P, 512], F32, name="xt%d_%d" % (p, bb), tag="bank")
                xts[p, bb] = xt
                for aa in range(2):
                    for u2 in range(2):
                        a = 2 * bb + aa
                        nc.tensor.transpose(
                            xt[:, u2 * 256 + aa * P: u2 * 256 + aa * P + P],
                            xf[:, a * 256 + u2 * P: a * 256 + u2 * P + P],
                            ident[:],
                        )

        def evac_t(p, bb, eng="v"):
            if p not in grp:
                grp[p] = grpool.tile([P, 2048], BF16, name="grp%d" % p, tag="grp", align_bytes=64)
            gf = grp[p][:].bitcast(F32).rearrange("p (c u) -> p c u", u=2)
            dst = gf[:, bb * 256:(bb + 1) * 256, :]
            src = xts[p, bb][:].rearrange("p (u c) -> p c u", u=2)
            if eng == "a":
                nc.scalar.copy(out=dst, in_=src)
            else:
                nc.vector.tensor_copy(out=dst, in_=src)

        def q1(p):
            ct = copool.tile([P, 512], U32, name="cod%d" % p, tag="cod", align_bytes=64)
            pt = copool.tile([P, 512], U8, name="pln%d" % p, tag="pln", align_bytes=64)
            nc.vector.quantize_mx(out=ct[:].bitcast(FP8X4), scales=pt[:], in_=grp[p][:])
            cod[p] = ct
            pln[p] = pt

        def slot_ops(s):
            g, r = divmod(s, 4)
            au, aw = ((0, 0), (0, 1), (1, 1), (1, 0))[r]
            return g, au, aw, 4 * g + (0, 3)[au], 4 * g + (1, 2)[aw]

        def mx1(s, nq):
            g, au, aw, pu, pw = slot_ops(s)
            pp = psb.tile([P, 512], F32, name="pp%d_%d" % (s, nq), tag="bank")
            for j in range(4):
                nc.tensor.matmul_mx(
                    out=pp[:, j * P:(j + 1) * P],
                    lhsT=cod[pu][:, j * P:(j + 1) * P].bitcast(FP8X4),
                    lhsT_scale=pln[pu][:, j * P:(j + 1) * P],
                    rhs=cod[pw][:, nq * P:(nq + 1) * P].bitcast(FP8X4),
                    rhs_scale=pln[pw][:, nq * P:(nq + 1) * P],
                    start=True,
                    stop=True,
                )
            xts[s, nq, "p"] = pp

        def evac_p(s, nq, eng="a"):
            if s not in pgt:
                pgt[s] = pgpool.tile([P, 2048], BF16, name="pg%d" % s, tag="pg", align_bytes=64)
            dst = pgt[s][:, nq * 512:(nq + 1) * 512].rearrange("p (n j) -> p n j", j=4)
            src = xts[s, nq, "p"][:].rearrange("p (j n) -> p n j", j=4)
            if eng == "a":
                nc.scalar.copy(out=dst, in_=src)
            else:
                nc.vector.tensor_copy(out=dst, in_=src)

        def q2(s, lo=0, hi=512):
            if s not in pcd:
                pcd[s] = pcpool.tile([P, 512], U32, name="pcd%d" % s, tag="pcd", align_bytes=64)
                ppl[s] = pcpool.tile([P, 512], U8, name="ppl%d" % s, tag="ppl", align_bytes=64)
            nc.vector.quantize_mx(out=pcd[s][:, lo:hi].bitcast(FP8X4), scales=ppl[s][:, lo:hi], in_=pgt[s][:, 4 * lo:4 * hi])

        def mx2(s, lo=0, hi=512):
            g, au, aw, pu, pw = slot_ops(s)
            un = 2 * g + au
            nc.tensor.matmul_mx(
                out=s_acc[aw][:, lo:hi],
                lhsT=ccodes[:, un * P:(un + 1) * P].bitcast(FP8X4),
                lhsT_scale=cplane[:, un * P:(un + 1) * P],
                rhs=pcd[s][:, lo:hi].bitcast(FP8X4),
                rhs_scale=ppl[s][:, lo:hi],
                start=(un == 0),
                stop=(un == NUNIT - 1 and hi == 512),
            )

        def b_unit(un):
            q, gl = divmod(un, 4)
            return bsb[q][:, gl * 512:(gl + 1) * 512]

        def max_unit(un):
            nc.vector.tensor_reduce(
                out=nmx[:, 4 * un:4 * un + 4], in_=b_unit(un).rearrange("p (r o) -> p r o", o=NO),
                axis=AX.X, op=ALU.max, negate=True,
            )

        def max_level(lo, hi, level):
            q = lo // 4
            nr = 4 * (hi - lo)
            if level == 0:
                src = bsb[q][:, (lo - 4 * q) * 512:(hi - 4 * q) * 512].rearrange("p (r o) -> p r o", o=NO)
            else:
                src = tree[lo, level - 1][:, 0:nr, :]
            w = NO >> (level + 1)
            if level == 4:
                nc.vector.tensor_reduce(out=nmx[:, 4 * lo:4 * hi], in_=src, axis=AX.X, op=ALU.max, negate=True)
            else:
                m = mpool.tile([P, 16, w], BF16, name="m%d_%d" % (level, lo), tag="m%d" % level)
                nc.vector.tensor_tensor(out=m[:, 0:nr, :], in0=src[:, :, 0:w], in1=src[:, :, w:2 * w], op=ALU.max)
                tree[lo, level] = m

        def sm_exp(e):
            un, j = divmod(e, 4)
            if j == 0:
                etl[un] = epool.tile([P, 512], F32, name="etl%d" % un, tag="etl")
                if un % 2 == 0:
                    sums[un // 2] = small.tile([P, 8], F32, name="sums%d" % un, tag="sums")
            k = 4 * (un % 2) + j
            nc.scalar.activation(
                out=etl[un][:, j * NO:(j + 1) * NO], in_=b_unit(un)[:, j * NO:(j + 1) * NO],
                func=ACTF.Exp, bias=nmx[:, e:e + 1], scale=1.0,
                accum_out=sums[un // 2][:, k:k + 1],
            )

        def sm_rec(g):
            rs = small.tile([P, 8], F32, name="rs%d" % g, tag="rs")
            nc.vector.reciprocal(out=rs[:], in_=sums[g][:])
            rcp[g] = rs

        def sm_half(k):
            un, h = divmod(k, 2)
            g, u = divmod(un, 2)
            cg = cgpool.tile([P, 256], BF16, name="cg%d" % k, tag="cg", align_bytes=64)
            nc.gpsimd.tensor_tensor(
                out=cg[:].rearrange("p (c i j) -> p c j i", i=4, j=4),
                in0=etl[un][:].rearrange("p (j c i) -> p c j i", j=4, i=4)[:, h * 16:(h + 1) * 16, :, :],
                in1=rcp[g][:, 4 * u:4 * u + 4].unsqueeze(1).unsqueeze(3).to_broadcast([P, 16, 4, 4]),
                op=ALU.mult,
            )
            cgt[k] = cg

        def sm_qh(k):
            nc.vector.quantize_mx(
                out=ccodes[:, k * 64:(k + 1) * 64].bitcast(FP8X4),
                scales=cplane[:, k * 64:(k + 1) * 64],
                in_=cgt[k][:],
            )

        n2 = [const.tile([P, 1], F32, name="n2_%d" % a) for a in range(2)]
        n1e = const.tile([P, 1], F32, name="n1e")
        n1p = const.tile([P, 1], F32, name="n1p")
        mhalf = const.tile([P, 1], F32, name="mhalf")

        nc.vector.memset(dum[:], 1.0)
        nc.vector.memset(mhalf[:], -0.5)
        nc.scalar.activation(out=dum2[:], in_=dum[:], func=ACTF.Exp)
        make_identity(nc, ident[:])
        load_b(0, 1)
        load_b(1, 2)
        load(0, 2)
        load(1, 2)
        load_b(2, 4)
        load(2)
        load(3)
        load_b(4, 8)
        load(4)
        load(5)
        load(6)
        load_b(8, 12)
        load(7)
        load(8)
        load(9)
        load_b(12, 16)
        for p in range(10, NB):
            load(p)
        max_unit(0)
        max_unit(1)
        for e in range(4):
            sm_exp(e)
        transposes(0)
        transposes(1)
        evac_t(0, 0)
        evac_t(0, 1, "a")
        evac_t(1, 0)
        evac_t(1, 1, "a")
        for e in range(4, 8):
            sm_exp(e)
        transposes(2)
        q1(0)
        max_level(2, 4, 0)
        q1(1)
        max_level(2, 4, 1)
        evac_t(2, 0, "a")
        max_level(2, 4, 2)
        evac_t(2, 1, "a")
        max_level(2, 4, 3)
        max_level(2, 4, 4)
        sm_rec(0)
        sm_half(0)
        done = 8
        MAXQ = {}
        for i, t0 in ((1, 0), (2, 8), (3, 16)):
            for l in range(5):
                MAXQ[t0 * 2 + l] = (4 * i, 4 * i + 4, l)

        def tree_piece(n):
            if n in MAXQ:
                max_level(*MAXQ[n])

        for t in range(0, NSLOT + M2LAG):
            k = t + 1
            if t + 3 < NPREP:
                transposes(t + 3)
                if t + NB < NPREP:
                    load(t + NB)
            if 0 <= t - M2LAG < NSLOT - 1:
                mx2(t - M2LAG)
            if t - M2LAG == NSLOT - 1:
                mx2(NSLOT - 1, 0, 256)
                mx2(NSLOT - 1, 256, 512)
            if t < NSLOT:
                for nq in range(4):
                    mx1(t, nq)
            upto = min(64, 12 + 2 * t)
            for e in range(done, upto):
                sm_exp(e)
            done = max(done, upto)
            if t < NSLOT:
                for nq in range(4):
                    if ("avaa"[nq] if t == NSLOT - 1 else "aaav"[nq] if t >= NSLOT - 4 else "a") == "a":
                        evac_p(t, nq)
            if t + 3 < NPREP:
                evac_t(t + 3, 0)
                evac_t(t + 3, 1)
            tree_piece(2 * t)
            if t == NSLOT - 1:
                evac_p(t, 1, "v")
            if t + 2 < NPREP:
                q1(t + 2)
            tree_piece(2 * t + 1)
            if t < 2 * NUNIT:
                sm_qh(t)
            if k % 4 == 0 and k // 4 < NS:
                sm_rec(k // 4)
            if k < 2 * NUNIT:
                sm_half(k)
            if 0 <= t - 1 < NSLOT - 1:
                q2(t - 1)
            if t < NSLOT:
                for nq in range(4):
                    if ("avaa"[nq] if t == NSLOT - 1 else "aaav"[nq] if t >= NSLOT - 4 else "a") == "v" and (t, nq) != (NSLOT - 1, 1):
                        evac_p(t, nq, "v")
            if t == NSLOT - 1:
                q2(t, 0, 256)
                q2(t, 256, 512)
            if t - M2LAG == NSLOT - 2:
                nc.scalar.activation(out=junk[:], in_=s_acc[1][:], func=ACTF.Square, accum_out=n2[1][:])
                nc.vector.tensor_scalar(out=n1e[:], in0=n2[1][:], scalar1=EPS, scalar2=None, op0=ALU.add)
                nc.vector.tensor_scalar(out=n1p[:], in0=n2[1][:], scalar1=1.0, scalar2=None, op0=ALU.add)

        nc.scalar.activation(out=junk[:], in_=s_acc[0][:], func=ACTF.Square, accum_out=n2[0][:])
        rr = const.tile([P, 1], F32, name="rr")
        n2e = const.tile([P, 1], F32, name="n2e")
        den = const.tile([P, 1], F32, name="den")
        rden = const.tile([P, 1], F32, name="rden")
        mfac = const.tile([P, 1], F32, name="mfac")
        fac = const.tile([P, 1], F32, name="fac")
        nc.gpsimd.tensor_tensor(out=n2e[:], in0=n2[0][:], in1=n1e[:], op=ALU.add)
        nc.gpsimd.tensor_tensor(out=rr[:], in0=n2e[:], in1=mhalf[:], op=ALU.pow)
        nc.vector.tensor_tensor(out=den[:], in0=n2[0][:], in1=n1p[:], op=ALU.add)
        nc.vector.reciprocal(out=rden[:], in_=den[:])
        nc.vector.scalar_tensor_tensor(out=mfac[:], in0=n2[0][:], scalar=n2[1][:, 0:1], in1=rden[:], op0=ALU.add, op1=ALU.mult)
        nc.scalar.activation(out=fac[:], in_=mfac[:], func=ACTF.Copy, scale=rr[:, 0:1])
        for h in range(2):
            for a in (1, 0):
                lo = a * 512 + h * 256
                dst = out_sb[:, lo:lo + 256].rearrange("p (c q) -> p c q", q=4)
                src = s_acc[a][:].rearrange("p (q c) -> p c q", q=4)[:, h * 64:(h + 1) * 64, :]
                if a == 0:
                    nc.scalar.activation(out=dst, in_=src, func=ACTF.Copy, scale=fac[:, 0:1])
                else:
                    nc.vector.tensor_scalar(out=dst, in0=src, scalar1=mfac[:, 0:1], scalar2=rr[:, 0:1], op0=ALU.mult, op1=ALU.mult)
                nc.sync.dma_start(out=out[:, lo:lo + 256], in_=out_sb[:, lo:lo + 256])
